import numpy as np
import ml_dtypes


def mxq(x, axis, fmt="e4m3"):
    dtype, down = {"e4m3": (ml_dtypes.float8_e4m3fn, 7), "e5m2": (ml_dtypes.float8_e5m2, 14)}[fmt]
    v = np.moveaxis(np.asarray(x, np.float32).astype(ml_dtypes.bfloat16).astype(np.float64), axis, -1)
    blocks = v.reshape(v.shape[:-1] + (-1, 32))
    amax = np.abs(blocks).max(-1, keepdims=True)
    byte = np.maximum(np.where(amax > 0, np.frexp(amax)[1] - 1 + 127, 0) - down, 1)
    scale = np.exp2(byte - 127.0)
    codes = (blocks / scale).astype(np.float32).astype(dtype).astype(np.float64)
    return np.moveaxis((codes * scale).reshape(v.shape), -1, axis)


WIDE = False


def mx_kscale(k):
    if not WIDE:
        return np.ones(k)
    levels = np.array([10, -10, 5, -5, 0])
    a = np.random.permutation(np.resize(levels, k // 512 * 4)).reshape(k // 512, 4)
    idx = np.arange(k)
    return np.exp2(a[idx // 512, idx % 128 // 32])


BF16 = ml_dtypes.bfloat16


def bf(x):
    return np.asarray(x, np.float32).astype(BF16)


def f64(x):
    return np.asarray(x).astype(np.float64)


B, S, HID, H, HK, D = 4, 2048, 512, 2, 2, 64
EPS = 1e-6
PRE = 0.004


def rmsnorm(v, w):
    var = np.mean(v * v, axis=-1, keepdims=True)
    return w * (v * (1.0 / np.sqrt(var + EPS)))


def rope(v, cos, sin):
    c = cos[:, :, None, :]
    sn = sin[:, :, None, :]
    v1, v2 = np.split(v, 2, axis=-1)
    rot = np.concatenate([-v2, v1], axis=-1)
    return v * c + rot * sn


def setup_inputs():
    s = mx_kscale(HID)
    return {
        "hidden_states": bf(np.random.standard_normal((B, S, HID)) * s),
        "cos": bf(np.cos(np.random.standard_normal((B, S, D)))),
        "sin": bf(np.sin(np.random.standard_normal((B, S, D)))),
        "Wq_query": bf(np.random.standard_normal((H * D, HID)) * PRE / np.sqrt(HID) / s),
        "Wk": bf(np.random.standard_normal((HK * D, HID)) * PRE / np.sqrt(HID) / s),
        "q_norm_w": bf(1.0 + 0.1 * np.random.standard_normal(D)),
        "k_norm_w": bf(1.0 + 0.1 * np.random.standard_normal(D)),
    }


def reference(hidden_states, cos, sin, Wq_query, Wk, q_norm_w, k_norm_w):
    xq = mxq(f64(hidden_states), 2, "e4m3")
    q = (xq @ mxq(f64(Wq_query), 1, "e4m3").T).reshape(B, S, H, D)
    k = (xq @ mxq(f64(Wk), 1, "e4m3").T).reshape(B, S, HK, D)
    q = rmsnorm(q, f64(q_norm_w))
    k = rmsnorm(k, f64(k_norm_w))
    q = rope(q, f64(cos), f64(sin))
    k = rope(k, f64(cos), f64(sin))
    return q, k

@@ -1,0 +1,252 @@
+from contextlib import ExitStack
+
+import concourse.bass as bass
+import concourse.mybir as mybir
+import concourse.tile as tile
+from concourse.masks import make_identity
+
+F32 = mybir.dt.float32
+BF16 = mybir.dt.bfloat16
+U32 = mybir.dt.uint32
+U8 = mybir.dt.uint8
+FP8X4 = mybir.dt.float8_e4m3fn_x4
+ALU = mybir.AluOpType
+ACT = mybir.ActivationFunctionType
+
+P = 128
+HID = 512
+D = 64
+HALF = 32
+NT = 64
+GT = 4
+NG = NT // GT
+CST = 16
+EPS = 1e-6
+FLOPS = 2 * 8192 * 512 * 256
+MANUAL = True
+K_ON_GPSIMD = False
+
+
+def tile_qwen3nextattentionforengine_pa_t_kernel(
+    tc, hidden_states, cos, sin, Wq_query, Wk, q_norm_w, k_norm_w, out_0, out_1
+):
+    nc = tc.nc
+    x_v = hidden_states.rearrange("b (s c) k -> (b s) c k", c=NT)
+    cos_v = cos.rearrange("b (s c) j -> (b s) c j", c=NT)
+    sin_v = sin.rearrange("b (s c) j -> (b s) c j", c=NT)
+    out_v = [
+        out_0.rearrange("b (s c) h d -> (b s) c (h d)", c=NT),
+        out_1.rearrange("b (s c) h d -> (b s) c (h d)", c=NT),
+    ]
+
+    with ExitStack() as ctx:
+        const = ctx.enter_context(tc.tile_pool(name="const", bufs=1))
+        xp = ctx.enter_context(tc.tile_pool(name="xp", bufs=NG))
+        csp = ctx.enter_context(tc.tile_pool(name="csp", bufs=NT // CST))
+        tbp = ctx.enter_context(tc.tile_pool(name="tbp", bufs=6))
+        grp = ctx.enter_context(tc.tile_pool(name="grp", bufs=3))
+        cdp = ctx.enter_context(tc.tile_pool(name="cdp", bufs=3))
+        stp = ctx.enter_context(tc.tile_pool(name="stp", bufs=4))
+        ttp = ctx.enter_context(tc.tile_pool(name="ttp", bufs=3))
+        outp = ctx.enter_context(tc.tile_pool(name="outp", bufs=4))
+        ps_t = ctx.enter_context(tc.psum_pool(name="ps_t", bufs=4))
+        ps_m = ctx.enter_context(tc.psum_pool(name="ps_m", bufs=4))
+        if MANUAL:
+            ctx.enter_context(tc.manual_schedule())
+
+        eps_t = const.tile([P, 1], F32)
+        nc.vector.memset(eps_t[:], EPS)
+        warm = const.tile([P, 1], F32)
+        nc.scalar.activation(out=warm[:], in_=eps_t[:], func=ACT.Sqrt)
+        ident = const.tile([P, P], F32)
+        make_identity(nc, ident[:])
+
+        w_sb = const.tile([P, 2 * HID], BF16)
+        nc.scalar.dma_start(out=w_sb[:, 0:HID], in_=Wq_query)
+        nc.scalar.dma_start(out=w_sb[:, HID : 2 * HID], in_=Wk)
+        wbf = const.tile([P, 2, D], BF16)
+        nc.scalar.dma_start(out=wbf[:, 0, :], in_=q_norm_w.partition_broadcast(P))
+        nc.scalar.dma_start(out=wbf[:, 1, :], in_=k_norm_w.partition_broadcast(P))
+
+        x_sb = []
+        cos_sb = []
+        sin_sb = []
+        for g in range(NG):
+            xg = xp.tile([P, GT * HID], BF16, name="xg")
+            nc.sync.dma_start(
+                out=xg[:].rearrange("p (c k) -> p c k", c=GT), in_=x_v[:, g * GT : (g + 1) * GT, :]
+            )
+            x_sb.append(xg)
+            if g % (CST // GT) == 0:
+                c0 = g * GT
+                cs = csp.tile([P, CST * D], BF16, name="cos_c")
+                nc.sync.dma_start(
+                    out=cs[:].rearrange("p (c j) -> p c j", c=CST), in_=cos_v[:, c0 : c0 + CST, :]
+                )
+                sn = csp.tile([P, CST * D], BF16, name="sin_c")
+                nc.sync.dma_start(
+                    out=sn[:].rearrange("p (c j) -> p c j", c=CST), in_=sin_v[:, c0 : c0 + CST, :]
+                )
+                cos_sb.append(cs)
+                sin_sb.append(sn)
+
+        wall = const.tile([P, 2, 2, D], F32)
+        nc.vector.tensor_copy(out=wall[:, 0, :, :], in_=wbf[:])
+        nc.vector.tensor_copy(out=wall[:, 1, :, 0:HALF], in_=wbf[:, :, 0:HALF])
+        nc.vector.tensor_scalar(
+            out=wall[:, 1, :, HALF:D], in0=wbf[:, :, HALF:D], scalar1=-1.0, scalar2=None, op0=ALU.mult
+        )
+
+        w_f = w_sb[:].bitcast(F32)
+        wt = ps_t.tile([P, 512], F32, name="xt")
+        for i in range(4):
+            nc.tensor.transpose(wt[:, i * P : (i + 1) * P], w_f[:, i * P : (i + 1) * P], ident[:])
+        w_gr = const.tile([P, 1024], BF16, align_bytes=64)
+        nc.vector.tensor_copy(
+            out=w_gr[:].bitcast(F32).rearrange("p (t f u) -> p t f u", t=2, u=2),
+            in_=wt[:].rearrange("p (t u f) -> p t f u", t=2, u=2),
+        )
+        w_codes = const.tile([P, 256], U32, align_bytes=64)
+        w_scales = const.tile([P, 256], U8, align_bytes=64)
+        nc.vector.quantize_mx(out=w_codes[:].bitcast(FP8X4), scales=w_scales[:], in_=w_gr[:])
+
+        junk = const.tile([P, D], BF16)
+
+        st = {}
+
+        def stage_tab(g):
+            tb = tbp.tile([P, GT * 256], F32, name="tb")
+            tbv = tb[:].rearrange("p (t y r j) -> p t y r j", t=GT, y=2, r=2)
+            lo = (g % (CST // GT)) * GT * D
+            cg = cos_sb[g // (CST // GT)][:, lo : lo + GT * D].rearrange("p (t j) -> p t j", t=GT)
+            sg = sin_sb[g // (CST // GT)][:, lo : lo + GT * D].rearrange("p (t j) -> p t j", t=GT)
+            nc.gpsimd.tensor_tensor(
+                out=tbv[:, :, :, 0, :],
+                in0=cg.unsqueeze(2).to_broadcast([P, GT, 2, D]),
+                in1=wall[:, 0, :, :].unsqueeze(1).to_broadcast([P, GT, 2, D]),
+                op=ALU.mult,
+            )
+            for half in range(2):
+                a = half * HALF
+                b = (1 - half) * HALF
+                nc.gpsimd.tensor_tensor(
+                    out=tbv[:, :, :, 1, a : a + HALF],
+                    in0=sg[:, :, b : b + HALF].unsqueeze(2).to_broadcast([P, GT, 2, HALF]),
+                    in1=wall[:, 1, :, a : a + HALF].unsqueeze(1).to_broadcast([P, GT, 2, HALF]),
+                    op=ALU.mult,
+                )
+            st[("tb", g)] = tb
+
+        def stage_a(g):
+            x_f = x_sb[g][:].bitcast(F32)
+            for h in range(2):
+                xt = ps_t.tile([P, 512], F32, name="xt")
+                for i in range(4):
+                    c = h * 512 + i * P
+                    nc.tensor.transpose(xt[:, i * P : (i + 1) * P], x_f[:, c : c + P], ident[:])
+                st[("xt", g, h)] = xt
+
+        def stage_b(g):
+            gr = grp.tile([P, GT * 512], BF16, name="gr", align_bytes=64)
+            gr_f = gr[:].bitcast(F32)
+            for h in range(2):
+                nc.scalar.copy(
+                    out=gr_f[:, h * 512 : (h + 1) * 512].rearrange("p (t r u) -> p t r u", t=2, u=2),
+                    in_=st[("xt", g, h)][:].rearrange("p (t u r) -> p t r u", t=2, u=2),
+                )
+            st[("gr", g)] = gr
+
+        def stage_c(g):
+            codes = cdp.tile([P, GT * P], U32, name="codes", align_bytes=64)
+            scales = cdp.tile([P, GT * P], U8, name="scales", align_bytes=64)
+            nc.vector.quantize_mx(out=codes[:].bitcast(FP8X4), scales=scales[:], in_=st[("gr", g)][:])
+            st[("cd", g)] = (codes, scales)
+
+        def stage_d(g):
+            codes, scales = st[("cd", g)]
+            for h in range(2):
+                mm = ps_m.tile([P, 512], F32, name="mm")
+                for t in range(2):
+                    c = (h * 2 + t) * P
+                    nc.tensor.matmul_mx(
+                        out=mm[:, t * 256 : (t + 1) * 256],
+                        lhsT=codes[:, c : c + P].bitcast(FP8X4),
+                        lhsT_scale=scales[:, c : c + P],
+                        rhs=w_codes[:].bitcast(FP8X4),
+                        rhs_scale=w_scales[:],
+                        start=True,
+                        stop=True,
+                    )
+                st[("mm", g, h)] = mm
+
+        def stage_e(g):
+            ss = stp.tile([P, GT * 4], F32, name="ss")
+            for h in range(2):
+                mm = st[("mm", g, h)]
+                for i in range(8):
+                    idx = h * 8 + i
+                    nc.scalar.activation(
+                        out=junk[:],
+                        in_=mm[:, i * D : (i + 1) * D],
+                        func=ACT.Square,
+                        accum_out=ss[:, idx : idx + 1],
+                    )
+            std = stp.tile([P, GT * 4], F32, name="std")
+            nc.scalar.activation(out=std[:], in_=ss[:], func=ACT.Sqrt, scale=1.0 / D, bias=eps_t[:, 0:1])
+            st[("std", g)] = std
+
+        def stage_f(g):
+            rstd = stp.tile([P, GT * 4], F32, name="rstd")
+            nc.vector.reciprocal(out=rstd[:], in_=st[("std", g)][:])
+            tt = ttp.tile([P, GT * 4 * 2 * D], F32, name="tt")
+            tb = st[("tb", g)]
+            for h in range(2):
+                mm = st[("mm", g, h)]
+                for i in range(8):
+                    idx = h * 8 + i
+                    tbi = (idx // 4) * 2 + (idx % 4) // 2
+                    nc.vector.scalar_tensor_tensor(
+                        out=tt[:, idx * 128 : (idx + 1) * 128].rearrange("p (r j) -> p r j", r=2),
+                        in0=mm[:, i * D : (i + 1) * D].unsqueeze(1).to_broadcast([P, 2, D]),
+                        scalar=rstd[:, idx : idx + 1],
+                        in1=tb[:, tbi * 128 : (tbi + 1) * 128].rearrange("p (r j) -> p r j", r=2),
+                        op0=ALU.mult,
+                        op1=ALU.mult,
+                    )
+            st[("tt", g)] = tt
+
+        def stage_h(g):
+            ttv = st[("tt", g)][:].rearrange("p (t y h r j) -> p t y h r j", t=GT, y=2, h=2, r=2)
+            for y in range(2):
+                o = outp.tile([P, GT * 128], F32, name="o%d" % y)
+                ov = o[:].rearrange("p (t h j) -> p t h j", t=GT, h=2)
+                eng = nc.gpsimd if (y == 1 and K_ON_GPSIMD) else nc.vector
+                for half in range(2):
+                    a = half * HALF
+                    b = (1 - half) * HALF
+                    eng.tensor_tensor(
+                        out=ov[:, :, :, a : a + HALF],
+                        in0=ttv[:, :, y, :, 0, a : a + HALF],
+                        in1=ttv[:, :, y, :, 1, b : b + HALF],
+                        op=ALU.add,
+                    )
+                nc.sync.dma_start(
+                    out=out_v[y][:, g * GT : (g + 1) * GT, :],
+                    in_=o[:].rearrange("p (t f) -> p t f", t=GT),
+                )
+
+        for i in range(NG + 3):
+            if i < NG:
+                stage_tab(i)
+                stage_a(i)
+            if 0 <= i - 1 < NG:
+                stage_c(i - 1)
+                stage_d(i - 1)
+            if 0 <= i - 2 < NG:
+                stage_e(i - 2)
+            if i < NG:
+                stage_b(i)
+            if 0 <= i - 3 < NG:
+                stage_h(i - 3)
+            if 0 <= i - 2 < NG:
+                stage_f(i - 2)

@@ -110,7 +110,6 @@ def tile_qwen3nextattentionforengine_pa_t_kernel(
         w_scales = const.tile([P, 256], U8, align_bytes=64)
         nc.vector.quantize_mx(out=w_codes[:].bitcast(FP8X4), scales=w_scales[:], in_=w_gr[:])
 
-        junk = const.tile([P, D], BF16)
 
         st = {}
 
@@ -181,12 +180,13 @@ def tile_qwen3nextattentionforengine_pa_t_kernel(
 
         def stage_e(g):
             ss = stp.tile([P, GT * 4], F32, name="ss")
+            junk = stp.tile([P, GT * 4 * D], BF16, name="junk")
             for h in range(2):
                 mm = st[("mm", g, h)]
                 for i in range(8):
                     idx = h * 8 + i
                     nc.scalar.activation(
-                        out=junk[:],
+                        out=junk[:, idx * D : (idx + 1) * D],
                         in_=mm[:, i * D : (i + 1) * D],
                         func=ACT.Square,
                         accum_out=ss[:, idx : idx + 1],

@@ -1,8 +1,6 @@
 from contextlib import ExitStack
 
-import concourse.bass as bass
 import concourse.mybir as mybir
-import concourse.tile as tile
 from concourse.masks import make_identity
 
 F32 = mybir.dt.float32
@@ -21,10 +19,9 @@ NT = 64
 GT = 4
 NG = NT // GT
 CST = 16
+GPC = CST // GT
 EPS = 1e-6
 FLOPS = 2 * 8192 * 512 * 256
-MANUAL = True
-K_ON_GPSIMD = False
 
 
 def tile_qwen3nextattentionforengine_pa_t_kernel(
@@ -43,59 +40,63 @@ def tile_qwen3nextattentionforengine_pa_t_kernel(
         const = ctx.enter_context(tc.tile_pool(name="const", bufs=1))
         xp = ctx.enter_context(tc.tile_pool(name="xp", bufs=NG))
         csp = ctx.enter_context(tc.tile_pool(name="csp", bufs=NT // CST))
-        tbp = ctx.enter_context(tc.tile_pool(name="tbp", bufs=6))
         grp = ctx.enter_context(tc.tile_pool(name="grp", bufs=3))
         cdp = ctx.enter_context(tc.tile_pool(name="cdp", bufs=3))
+        sqp = ctx.enter_context(tc.tile_pool(name="sqp", bufs=4))
         stp = ctx.enter_context(tc.tile_pool(name="stp", bufs=4))
         ttp = ctx.enter_context(tc.tile_pool(name="ttp", bufs=3))
         outp = ctx.enter_context(tc.tile_pool(name="outp", bufs=4))
-        ps_t = ctx.enter_context(tc.psum_pool(name="ps_t", bufs=4))
-        ps_m = ctx.enter_context(tc.psum_pool(name="ps_m", bufs=4))
-        if MANUAL:
-            ctx.enter_context(tc.manual_schedule())
+        ps_t = ctx.enter_context(tc.psum_pool(name="ps_t", bufs=2))
+        ps_v = ctx.enter_context(tc.psum_pool(name="ps_v", bufs=2))
+        ps_u = ctx.enter_context(tc.psum_pool(name="ps_u", bufs=3))
+        ps_s = ctx.enter_context(tc.psum_pool(name="ps_s", bufs=1))
+        ctx.enter_context(tc.manual_schedule())
 
         eps_t = const.tile([P, 1], F32)
         nc.vector.memset(eps_t[:], EPS)
-        warm = const.tile([P, 1], F32)
-        nc.scalar.activation(out=warm[:], in_=eps_t[:], func=ACT.Sqrt)
         ident = const.tile([P, P], F32)
         make_identity(nc, ident[:])
+        ident_b = const.tile([P, P], BF16)
+        make_identity(nc, ident_b[:])
+        zrow = const.tile([P, P], BF16)
+        nc.vector.memset(zrow[:], 0.0)
+        ind = const.tile([P, 2], F32)
+        nc.vector.memset(ind[:], 0.0)
+        nc.vector.memset(ind[0:D, 0:1], 1.0 / D)
+        nc.vector.memset(ind[D:P, 1:2], 1.0 / D)
 
         w_sb = const.tile([P, 2 * HID], BF16)
         nc.scalar.dma_start(out=w_sb[:, 0:HID], in_=Wq_query)
         nc.scalar.dma_start(out=w_sb[:, HID : 2 * HID], in_=Wk)
-        wbf = const.tile([P, 2, D], BF16)
-        nc.scalar.dma_start(out=wbf[:, 0, :], in_=q_norm_w.partition_broadcast(P))
-        nc.scalar.dma_start(out=wbf[:, 1, :], in_=k_norm_w.partition_broadcast(P))
+        for y, gain in enumerate((q_norm_w, k_norm_w)):
+            row = gain.rearrange("(o d) -> o d", o=1)
+            nc.scalar.dma_start(out=zrow[y : y + 1, 0:D], in_=row)
+            nc.scalar.dma_start(out=zrow[y : y + 1, D:P], in_=row)
+        warm = const.tile([P, 1], F32)
+        nc.scalar.activation(out=warm[:], in_=eps_t[:], func=ACT.Sqrt)
 
         x_sb = []
-        cos_sb = []
-        sin_sb = []
+        cs_sb = []
+        sraw_sb = []
         for g in range(NG):
             xg = xp.tile([P, GT * HID], BF16, name="xg")
             nc.sync.dma_start(
                 out=xg[:].rearrange("p (c k) -> p c k", c=GT), in_=x_v[:, g * GT : (g + 1) * GT, :]
             )
             x_sb.append(xg)
-            if g % (CST // GT) == 0:
+            if g % GPC == 0:
                 c0 = g * GT
-                cs = csp.tile([P, CST * D], BF16, name="cos_c")
+                cs = csp.tile([P, 2 * CST * D], BF16, name="cs")
                 nc.sync.dma_start(
-                    out=cs[:].rearrange("p (c j) -> p c j", c=CST), in_=cos_v[:, c0 : c0 + CST, :]
+                    out=cs[:, 0 : CST * D].rearrange("p (c j) -> p c j", c=CST),
+                    in_=cos_v[:, c0 : c0 + CST, :],
                 )
-                sn = csp.tile([P, CST * D], BF16, name="sin_c")
+                sraw = csp.tile([P, CST * D], BF16, name="sraw")
                 nc.sync.dma_start(
-                    out=sn[:].rearrange("p (c j) -> p c j", c=CST), in_=sin_v[:, c0 : c0 + CST, :]
+                    out=sraw[:].rearrange("p (c j) -> p c j", c=CST), in_=sin_v[:, c0 : c0 + CST, :]
                 )
-                cos_sb.append(cs)
-                sin_sb.append(sn)
-
-        wall = const.tile([P, 2, 2, D], F32)
-        nc.vector.tensor_copy(out=wall[:, 0, :, :], in_=wbf[:])
-        nc.vector.tensor_copy(out=wall[:, 1, :, 0:HALF], in_=wbf[:, :, 0:HALF])
-        nc.vector.tensor_scalar(
-            out=wall[:, 1, :, HALF:D], in0=wbf[:, :, HALF:D], scalar1=-1.0, scalar2=None, op0=ALU.mult
-        )
+                cs_sb.append(cs)
+                sraw_sb.append(sraw)
 
         w_f = w_sb[:].bitcast(F32)
         wt = ps_t.tile([P, 512], F32, name="xt")
@@ -110,31 +111,24 @@ def tile_qwen3nextattentionforengine_pa_t_kernel(
         w_scales = const.tile([P, 256], U8, align_bytes=64)
         nc.vector.quantize_mx(out=w_codes[:].bitcast(FP8X4), scales=w_scales[:], in_=w_gr[:])
 
+        gt_ps = ps_t.tile([P, P], BF16, name="xt")
+        nc.tensor.transpose(gt_ps[:], zrow[:], ident_b[:])
+        wcol = const.tile([P, 2], F32)
+        nc.vector.tensor_copy(out=wcol[:], in_=gt_ps[:, 0:2])
 
         st = {}
 
-        def stage_tab(g):
-            tb = tbp.tile([P, GT * 256], F32, name="tb")
-            tbv = tb[:].rearrange("p (t y r j) -> p t y r j", t=GT, y=2, r=2)
-            lo = (g % (CST // GT)) * GT * D
-            cg = cos_sb[g // (CST // GT)][:, lo : lo + GT * D].rearrange("p (t j) -> p t j", t=GT)
-            sg = sin_sb[g // (CST // GT)][:, lo : lo + GT * D].rearrange("p (t j) -> p t j", t=GT)
-            nc.gpsimd.tensor_tensor(
-                out=tbv[:, :, :, 0, :],
-                in0=cg.unsqueeze(2).to_broadcast([P, GT, 2, D]),
-                in1=wall[:, 0, :, :].unsqueeze(1).to_broadcast([P, GT, 2, D]),
-                op=ALU.mult,
+        def stage_cs(k):
+            dst = cs_sb[k][:, CST * D : 2 * CST * D].rearrange("p (c j) -> p c j", c=CST)
+            src = sraw_sb[k][:].rearrange("p (c j) -> p c j", c=CST)
+            nc.gpsimd.tensor_scalar(
+                out=dst[:, :, 0:HALF], in0=src[:, :, HALF:D], scalar1=1.0, scalar2=0.0,
+                op0=ALU.mult, op1=ALU.add,
             )
-            for half in range(2):
-                a = half * HALF
-                b = (1 - half) * HALF
-                nc.gpsimd.tensor_tensor(
-                    out=tbv[:, :, :, 1, a : a + HALF],
-                    in0=sg[:, :, b : b + HALF].unsqueeze(2).to_broadcast([P, GT, 2, HALF]),
-                    in1=wall[:, 1, :, a : a + HALF].unsqueeze(1).to_broadcast([P, GT, 2, HALF]),
-                    op=ALU.mult,
-                )
-            st[("tb", g)] = tb
+            nc.gpsimd.tensor_scalar(
+                out=dst[:, :, HALF:D], in0=src[:, :, 0:HALF], scalar1=-1.0, scalar2=0.0,
+                op0=ALU.mult, op1=ALU.add,
+            )
 
         def stage_a(g):
             x_f = x_sb[g][:].bitcast(F32)
@@ -163,90 +157,125 @@ def tile_qwen3nextattentionforengine_pa_t_kernel(
 
         def stage_d(g):
             codes, scales = st[("cd", g)]
-            for h in range(2):
-                mm = ps_m.tile([P, 512], F32, name="mm")
-                for t in range(2):
-                    c = (h * 2 + t) * P
-                    nc.tensor.matmul_mx(
-                        out=mm[:, t * 256 : (t + 1) * 256],
-                        lhsT=codes[:, c : c + P].bitcast(FP8X4),
-                        lhsT_scale=scales[:, c : c + P],
-                        rhs=w_codes[:].bitcast(FP8X4),
-                        rhs_scale=w_scales[:],
+            for y in range(2):
+                vt = ps_v.tile([P, 512], F32, name="vt")
+                nc.tensor.matmul_mx(
+                    out=vt[:],
+                    lhsT=w_codes[:, y * P : (y + 1) * P].bitcast(FP8X4),
+                    lhsT_scale=w_scales[:, y * P : (y + 1) * P],
+                    rhs=codes[:].bitcast(FP8X4),
+                    rhs_scale=scales[:],
+                    start=True,
+                    stop=True,
+                )
+                st[("vt", g, y)] = vt
+
+        def stage_e(g):
+            for y in range(2):
+                vt = st[("vt", g, y)]
+                sq = sqp.tile([P, 512], F32, name="sq")
+                nc.scalar.activation(out=sq[:], in_=vt[:], func=ACT.Square)
+                ut = sqp.tile([P, 512], F32, name="ut")
+                nc.scalar.activation(out=ut[:], in_=vt[:], func=ACT.Copy, scale=wcol[:, y : y + 1])
+                st[("sq", g, y)] = sq
+                st[("ut", g, y)] = ut
+
+        def stage_m(g):
+            ssp = ps_s.tile([P, GT * 4], F32, name="ssp")
+            for y in range(2):
+                sq = st[("sq", g, y)]
+                for t in range(GT):
+                    k = t * 2 + y
+                    nc.tensor.matmul(
+                        out=ssp[:, k * 2 : (k + 1) * 2],
+                        lhsT=sq[:, t * P : (t + 1) * P],
+                        rhs=ind[:],
                         start=True,
                         stop=True,
                     )
-                st[("mm", g, h)] = mm
+            st[("ssp", g)] = ssp
 
-        def stage_e(g):
-            ss = stp.tile([P, GT * 4], F32, name="ss")
-            junk = stp.tile([P, GT * 4 * D], BF16, name="junk")
-            for h in range(2):
-                mm = st[("mm", g, h)]
-                for i in range(8):
-                    idx = h * 8 + i
-                    nc.scalar.activation(
-                        out=junk[:, idx * D : (idx + 1) * D],
-                        in_=mm[:, i * D : (i + 1) * D],
-                        func=ACT.Square,
-                        accum_out=ss[:, idx : idx + 1],
+        def stage_t(g, hb):
+            up = ps_u.tile([P, 512], F32, name="up")
+            for t2 in range(2):
+                for y in range(2):
+                    t = hb * 2 + t2
+                    c = t2 * 256 + y * P
+                    nc.tensor.transpose(
+                        up[:, c : c + P], st[("ut", g, y)][:, t * P : (t + 1) * P], ident[:]
                     )
+            st[("up", g, hb)] = up
+
+        def stage_r(g):
             std = stp.tile([P, GT * 4], F32, name="std")
-            nc.scalar.activation(out=std[:], in_=ss[:], func=ACT.Sqrt, scale=1.0 / D, bias=eps_t[:, 0:1])
+            nc.scalar.activation(out=std[:], in_=st[("ssp", g)][:], func=ACT.Sqrt, bias=eps_t[:, 0:1])
             st[("std", g)] = std
 
         def stage_f(g):
             rstd = stp.tile([P, GT * 4], F32, name="rstd")
             nc.vector.reciprocal(out=rstd[:], in_=st[("std", g)][:])
             tt = ttp.tile([P, GT * 4 * 2 * D], F32, name="tt")
-            tb = st[("tb", g)]
-            for h in range(2):
-                mm = st[("mm", g, h)]
-                for i in range(8):
-                    idx = h * 8 + i
-                    tbi = (idx // 4) * 2 + (idx % 4) // 2
-                    nc.vector.scalar_tensor_tensor(
-                        out=tt[:, idx * 128 : (idx + 1) * 128].rearrange("p (r j) -> p r j", r=2),
-                        in0=mm[:, i * D : (i + 1) * D].unsqueeze(1).to_broadcast([P, 2, D]),
-                        scalar=rstd[:, idx : idx + 1],
-                        in1=tb[:, tbi * 128 : (tbi + 1) * 128].rearrange("p (r j) -> p r j", r=2),
-                        op0=ALU.mult,
-                        op1=ALU.mult,
-                    )
+            csv = cs_sb[g // GPC][:].rearrange("p (r c j) -> p r c j", r=2, c=CST)
+            for hb in range(2):
+                up = st[("up", g, hb)]
+                for t2 in range(2):
+                    t = hb * 2 + t2
+                    for yh in range(4):
+                        si = t * 4 + yh
+                        ti = (yh // 2) * 8 + t * 2 + yh % 2
+                        c = t2 * 256 + yh * D
+                        nc.vector.scalar_tensor_tensor(
+                            out=tt[:, ti * 128 : (ti + 1) * 128].rearrange("p (r j) -> p r j", r=2),
+                            in0=up[:, c : c + D].unsqueeze(1).to_broadcast([P, 2, D]),
+                            scalar=rstd[:, si : si + 1],
+                            in1=csv[:, :, (g % GPC) * GT + t, :],
+                            op0=ALU.mult,
+                            op1=ALU.mult,
+                        )
             st[("tt", g)] = tt
 
         def stage_h(g):
-            ttv = st[("tt", g)][:].rearrange("p (t y h r j) -> p t y h r j", t=GT, y=2, h=2, r=2)
+            ttv = st[("tt", g)][:].rearrange("p (n r j) -> p n r j", r=2, j=D)
+            o = outp.tile([P, 2 * GT * 128], F32, name="o")
+            ov = o[:].rearrange("p (n j) -> p n j", j=D)
+            for half in range(2):
+                a = half * HALF
+                b = (1 - half) * HALF
+                nc.gpsimd.tensor_tensor(
+                    out=ov[:, :, a : a + HALF],
+                    in0=ttv[:, :, 0, a : a + HALF],
+                    in1=ttv[:, :, 1, b : b + HALF],
+                    op=ALU.add,
+                )
             for y in range(2):
-                o = outp.tile([P, GT * 128], F32, name="o%d" % y)
-                ov = o[:].rearrange("p (t h j) -> p t h j", t=GT, h=2)
-                eng = nc.gpsimd if (y == 1 and K_ON_GPSIMD) else nc.vector
-                for half in range(2):
-                    a = half * HALF
-                    b = (1 - half) * HALF
-                    eng.tensor_tensor(
-                        out=ov[:, :, :, a : a + HALF],
-                        in0=ttv[:, :, y, :, 0, a : a + HALF],
-                        in1=ttv[:, :, y, :, 1, b : b + HALF],
-                        op=ALU.add,
-                    )
                 nc.sync.dma_start(
                     out=out_v[y][:, g * GT : (g + 1) * GT, :],
-                    in_=o[:].rearrange("p (t f) -> p t f", t=GT),
+                    in_=o[:, y * GT * 128 : (y + 1) * GT * 128].rearrange("p (t f) -> p t f", t=GT),
                 )
 
+        def on(g):
+            return 0 <= g < NG
+
         for i in range(NG + 3):
-            if i < NG:
-                stage_tab(i)
-                stage_a(i)
-            if 0 <= i - 1 < NG:
+            if i % GPC == 0 and i < NG:
+                stage_cs(i // GPC)
+            if on(i - 3):
+                stage_r(i - 3)
+                stage_t(i - 3, 0)
+            if on(i - 1):
                 stage_c(i - 1)
-                stage_d(i - 1)
-            if 0 <= i - 2 < NG:
+            if on(i - 2):
                 stage_e(i - 2)
-            if i < NG:
-                stage_b(i)
-            if 0 <= i - 3 < NG:
+            if on(i - 3):
+                stage_t(i - 3, 1)
+                stage_f(i - 3)
+            if on(i):
+                stage_a(i)
+            if on(i - 3):
                 stage_h(i - 3)
-            if 0 <= i - 2 < NG:
-                stage_f(i - 2)
+            if on(i - 2):
+                stage_m(i - 2)
+            if on(i):
+                stage_b(i)
+            if on(i - 1):
+                stage_d(i - 1)

@@ -21,6 +21,7 @@ NG = NT // GT
 CST = 16
 GPC = CST // GT
 EPS = 1e-6
+NIND = 32
 FLOPS = 2 * 8192 * 512 * 256
 
 
@@ -60,7 +61,7 @@ def tile_qwen3nextattentionforengine_pa_t_kernel(
         make_identity(nc, ident_b[:])
         zrow = const.tile([P, P], BF16)
         nc.vector.memset(zrow[:], 0.0)
-        ind = const.tile([P, 2], F32)
+        ind = const.tile([P, NIND], F32)
         nc.vector.memset(ind[:], 0.0)
         nc.vector.memset(ind[0:D, 0:1], 1.0 / D)
         nc.vector.memset(ind[D:P, 1:2], 1.0 / D)
@@ -180,35 +181,38 @@ def tile_qwen3nextattentionforengine_pa_t_kernel(
                 st[("sq", g, y)] = sq
                 st[("ut", g, y)] = ut
 
-        def stage_m(g):
-            ssp = ps_s.tile([P, GT * 4], F32, name="ssp")
-            for y in range(2):
-                sq = st[("sq", g, y)]
-                for t in range(GT):
+        def stage_mt(g):
+            ssp = ps_s.tile([P, 2 * GT * NIND], F32, name="ssp")
+            ups = [ps_u.tile([P, 512], F32, name="up") for hb in range(2)]
+            for q in range(4):
+                for m in (2 * q, 2 * q + 1):
+                    y = m // GT
+                    t = m % GT
                     k = t * 2 + y
                     nc.tensor.matmul(
-                        out=ssp[:, k * 2 : (k + 1) * 2],
-                        lhsT=sq[:, t * P : (t + 1) * P],
+                        out=ssp[:, k * NIND : (k + 1) * NIND],
+                        lhsT=st[("sq", g, y)][:, t * P : (t + 1) * P],
                         rhs=ind[:],
                         start=True,
                         stop=True,
                     )
-            st[("ssp", g)] = ssp
-
-        def stage_t(g, hb):
-            up = ps_u.tile([P, 512], F32, name="up")
-            for t2 in range(2):
                 for y in range(2):
-                    t = hb * 2 + t2
-                    c = t2 * 256 + y * P
+                    c = (q % 2) * 256 + y * P
                     nc.tensor.transpose(
-                        up[:, c : c + P], st[("ut", g, y)][:, t * P : (t + 1) * P], ident[:]
+                        ups[q // 2][:, c : c + P], st[("ut", g, y)][:, q * P : (q + 1) * P], ident[:]
                     )
-            st[("up", g, hb)] = up
+            st[("ssp", g)] = ssp
+            st[("up", g, 0)] = ups[0]
+            st[("up", g, 1)] = ups[1]
 
         def stage_r(g):
             std = stp.tile([P, GT * 4], F32, name="std")
-            nc.scalar.activation(out=std[:], in_=st[("ssp", g)][:], func=ACT.Sqrt, bias=eps_t[:, 0:1])
+            nc.scalar.activation(
+                out=std[:].rearrange("p (k n) -> p k n", n=2),
+                in_=st[("ssp", g)][:].rearrange("p (k n) -> p k n", n=NIND)[:, :, 0:2],
+                func=ACT.Sqrt,
+                bias=eps_t[:, 0:1],
+            )
             st[("std", g)] = std
 
         def stage_f(g):
@@ -256,26 +260,24 @@ def tile_qwen3nextattentionforengine_pa_t_kernel(
         def on(g):
             return 0 <= g < NG
 
-        for i in range(NG + 3):
+        for i in range(NG + 5):
             if i % GPC == 0 and i < NG:
                 stage_cs(i // GPC)
-            if on(i - 3):
-                stage_r(i - 3)
-                stage_t(i - 3, 0)
-            if on(i - 1):
-                stage_c(i - 1)
-            if on(i - 2):
-                stage_e(i - 2)
-            if on(i - 3):
-                stage_t(i - 3, 1)
-                stage_f(i - 3)
             if on(i):
                 stage_a(i)
-            if on(i - 3):
-                stage_h(i - 3)
             if on(i - 2):
-                stage_m(i - 2)
-            if on(i):
-                stage_b(i)
+                stage_c(i - 2)
             if on(i - 1):
-                stage_d(i - 1)
+                stage_b(i - 1)
+            if on(i - 2):
+                stage_d(i - 2)
+            if on(i - 3):
+                stage_e(i - 3)
+            if on(i - 5):
+                stage_f(i - 5)
+            if on(i - 4):
+                stage_r(i - 4)
+            if on(i - 3):
+                stage_mt(i - 3)
+            if on(i - 5):
+                stage_h(i - 5)

@@ -21,7 +21,7 @@ NG = NT // GT
 CST = 16
 GPC = CST // GT
 EPS = 1e-6
-NIND = 32
+NIND = 48
 FLOPS = 2 * 8192 * 512 * 256
 
 

@@ -49,7 +49,8 @@ def tile_qwen3nextattentionforengine_pa_t_kernel(
         outp = ctx.enter_context(tc.tile_pool(name="outp", bufs=4))
         ps_t = ctx.enter_context(tc.psum_pool(name="ps_t", bufs=2))
         ps_v = ctx.enter_context(tc.psum_pool(name="ps_v", bufs=2))
-        ps_u = ctx.enter_context(tc.psum_pool(name="ps_u", bufs=3))
+        ps_u = ctx.enter_context(tc.psum_pool(name="ps_u", bufs=2))
+        ps_k = ctx.enter_context(tc.psum_pool(name="ps_k", bufs=1))
         ps_s = ctx.enter_context(tc.psum_pool(name="ps_s", bufs=1))
         ctx.enter_context(tc.manual_schedule())
 
@@ -74,7 +75,7 @@ def tile_qwen3nextattentionforengine_pa_t_kernel(
             nc.scalar.dma_start(out=zrow[y : y + 1, 0:D], in_=row)
             nc.scalar.dma_start(out=zrow[y : y + 1, D:P], in_=row)
         warm = const.tile([P, 1], F32)
-        nc.scalar.activation(out=warm[:], in_=eps_t[:], func=ACT.Sqrt)
+        nc.scalar.activation(out=warm[:], in_=eps_t[:], func=ACT.Abs_reciprocal_sqrt)
 
         x_sb = []
         cs_sb = []
@@ -170,54 +171,79 @@ def tile_qwen3nextattentionforengine_pa_t_kernel(
                     stop=True,
                 )
                 st[("vt", g, y)] = vt
+            mk = ps_k.tile([P, 512], F32, name="mk")
+            for t in range(GT):
+                nc.tensor.matmul_mx(
+                    out=mk[:, t * P : (t + 1) * P],
+                    lhsT=codes[:, t * P : (t + 1) * P].bitcast(FP8X4),
+                    lhsT_scale=scales[:, t * P : (t + 1) * P],
+                    rhs=w_codes[:, P : 2 * P].bitcast(FP8X4),
+                    rhs_scale=w_scales[:, P : 2 * P],
+                    start=True,
+                    stop=True,
+                )
+            st[("mk", g)] = mk
 
         def stage_e(g):
             for y in range(2):
                 vt = st[("vt", g, y)]
                 sq = sqp.tile([P, 512], F32, name="sq")
-                nc.scalar.activation(out=sq[:], in_=vt[:], func=ACT.Square)
+                nc.scalar.activation(out=sq[:], in_=(vt if y == 0 else st[("mk", g)])[:], func=ACT.Square)
                 ut = sqp.tile([P, 512], F32, name="ut")
                 nc.scalar.activation(out=ut[:], in_=vt[:], func=ACT.Copy, scale=wcol[:, y : y + 1])
                 st[("sq", g, y)] = sq
                 st[("ut", g, y)] = ut
 
         def stage_mt(g):
-            ssp = ps_s.tile([P, 2 * GT * NIND], F32, name="ssp")
+            ssp = ps_s.tile([P, GT * NIND], F32, name="ssp")
             ups = [ps_u.tile([P, 512], F32, name="up") for hb in range(2)]
-            for q in range(4):
-                for m in (2 * q, 2 * q + 1):
-                    y = m // GT
-                    t = m % GT
-                    k = t * 2 + y
-                    nc.tensor.matmul(
-                        out=ssp[:, k * NIND : (k + 1) * NIND],
-                        lhsT=st[("sq", g, y)][:, t * P : (t + 1) * P],
-                        rhs=ind[:],
-                        start=True,
-                        stop=True,
-                    )
+            for t in range(GT):
+                nc.tensor.matmul(
+                    out=ssp[:, t * NIND : (t + 1) * NIND],
+                    lhsT=st[("sq", g, 0)][:, t * P : (t + 1) * P],
+                    rhs=ind[:],
+                    start=True,
+                    stop=True,
+                )
                 for y in range(2):
-                    c = (q % 2) * 256 + y * P
+                    c = (t % 2) * 256 + y * P
                     nc.tensor.transpose(
-                        ups[q // 2][:, c : c + P], st[("ut", g, y)][:, q * P : (q + 1) * P], ident[:]
+                        ups[t // 2][:, c : c + P], st[("ut", g, y)][:, t * P : (t + 1) * P], ident[:]
                     )
             st[("ssp", g)] = ssp
             st[("up", g, 0)] = ups[0]
             st[("up", g, 1)] = ups[1]
 
+        def stage_rd(g):
+            ssv = stp.tile([P, GT * 2], F32, name="ssv")
+            nc.vector.tensor_reduce(
+                out=ssv[:],
+                in_=st[("sq", g, 1)][:].rearrange("p (n j) -> p n j", j=D),
+                axis=mybir.AxisListType.X,
+                op=ALU.add,
+            )
+            st[("ssv", g)] = ssv
+
         def stage_r(g):
-            std = stp.tile([P, GT * 4], F32, name="std")
+            rstd = stp.tile([P, GT * 4], F32, name="rstd")
+            rv = rstd[:].rearrange("p (t y h) -> p t y h", y=2, h=2)
             nc.scalar.activation(
-                out=std[:].rearrange("p (k n) -> p k n", n=2),
-                in_=st[("ssp", g)][:].rearrange("p (k n) -> p k n", n=NIND)[:, :, 0:2],
-                func=ACT.Sqrt,
+                out=rv[:, :, 0, :],
+                in_=st[("ssp", g)][:].rearrange("p (t n) -> p t n", n=NIND)[:, :, 0:2],
+                func=ACT.Abs_reciprocal_sqrt,
                 bias=eps_t[:, 0:1],
             )
-            st[("std", g)] = std
+            nc.scalar.activation(
+                out=rv[:, :, 1, :],
+                in_=st[("ssv", g)][:].rearrange("p (t h) -> p t h", h=2),
+                func=ACT.Abs_reciprocal_sqrt,
+                scale=1.0 / D,
+                bias=eps_t[:, 0:1],
+            )
+            st[("rstd", g)] = rstd
 
         def stage_f(g):
-            rstd = stp.tile([P, GT * 4], F32, name="rstd")
-            nc.vector.reciprocal(out=rstd[:], in_=st[("std", g)][:])
+            rstd = st[("rstd", g)]
             tt = ttp.tile([P, GT * 4 * 2 * D], F32, name="tt")
             csv = cs_sb[g // GPC][:].rearrange("p (r c j) -> p r c j", r=2, c=CST)
             for hb in range(2):
@@ -263,21 +289,21 @@ def tile_qwen3nextattentionforengine_pa_t_kernel(
         for i in range(NG + 5):
             if i % GPC == 0 and i < NG:
                 stage_cs(i // GPC)
-            if on(i):
-                stage_a(i)
-            if on(i - 2):
-                stage_c(i - 2)
-            if on(i - 1):
-                stage_b(i - 1)
-            if on(i - 2):
-                stage_d(i - 2)
             if on(i - 3):
                 stage_e(i - 3)
+            if on(i - 4):
+                stage_rd(i - 4)
+                stage_r(i - 4)
             if on(i - 5):
                 stage_f(i - 5)
-            if on(i - 4):
-                stage_r(i - 4)
+            if on(i - 2):
+                stage_c(i - 2)
+                stage_d(i - 2)
+            if on(i - 1):
+                stage_b(i - 1)
             if on(i - 3):
                 stage_mt(i - 3)
+            if on(i):
+                stage_a(i)
             if on(i - 5):
                 stage_h(i - 5)

@@ -21,6 +21,8 @@ NG = NT // GT
 CST = 16
 GPC = CST // GT
 EPS = 1e-6
+VT = 1
+PT = GT - VT
 NIND = 48
 FLOPS = 2 * 8192 * 512 * 256
 
@@ -171,14 +173,15 @@ def tile_qwen3nextattentionforengine_pa_t_kernel(
                     stop=True,
                 )
                 st[("vt", g, y)] = vt
-            mk = ps_k.tile([P, 512], F32, name="mk")
-            for t in range(GT):
+            mk = ps_k.tile([P, VT * 256], F32, name="mk")
+            for v in range(VT):
+                c = (PT + v) * P
                 nc.tensor.matmul_mx(
-                    out=mk[:, t * P : (t + 1) * P],
-                    lhsT=codes[:, t * P : (t + 1) * P].bitcast(FP8X4),
-                    lhsT_scale=scales[:, t * P : (t + 1) * P],
-                    rhs=w_codes[:, P : 2 * P].bitcast(FP8X4),
-                    rhs_scale=w_scales[:, P : 2 * P],
+                    out=mk[:, v * 256 : (v + 1) * 256],
+                    lhsT=codes[:, c : c + P].bitcast(FP8X4),
+                    lhsT_scale=scales[:, c : c + P],
+                    rhs=w_codes[:].bitcast(FP8X4),
+                    rhs_scale=w_scales[:],
                     start=True,
                     stop=True,
                 )
@@ -187,24 +190,30 @@ def tile_qwen3nextattentionforengine_pa_t_kernel(
         def stage_e(g):
             for y in range(2):
                 vt = st[("vt", g, y)]
-                sq = sqp.tile([P, 512], F32, name="sq")
-                nc.scalar.activation(out=sq[:], in_=(vt if y == 0 else st[("mk", g)])[:], func=ACT.Square)
+                sq = sqp.tile([P, PT * P], F32, name="sq")
+                nc.scalar.activation(out=sq[:], in_=vt[:, 0 : PT * P], func=ACT.Square)
                 ut = sqp.tile([P, 512], F32, name="ut")
                 nc.scalar.activation(out=ut[:], in_=vt[:], func=ACT.Copy, scale=wcol[:, y : y + 1])
                 st[("sq", g, y)] = sq
                 st[("ut", g, y)] = ut
+            sk = sqp.tile([P, VT * 256], F32, name="sk")
+            nc.scalar.activation(out=sk[:], in_=st[("mk", g)][:], func=ACT.Square)
+            st[("sk", g)] = sk
 
         def stage_mt(g):
-            ssp = ps_s.tile([P, GT * NIND], F32, name="ssp")
+            ssp = ps_s.tile([P, 2 * PT * NIND], F32, name="ssp")
             ups = [ps_u.tile([P, 512], F32, name="up") for hb in range(2)]
             for t in range(GT):
-                nc.tensor.matmul(
-                    out=ssp[:, t * NIND : (t + 1) * NIND],
-                    lhsT=st[("sq", g, 0)][:, t * P : (t + 1) * P],
-                    rhs=ind[:],
-                    start=True,
-                    stop=True,
-                )
+                for y in range(2):
+                    if t < PT:
+                        k = t * 2 + y
+                        nc.tensor.matmul(
+                            out=ssp[:, k * NIND : (k + 1) * NIND],
+                            lhsT=st[("sq", g, y)][:, t * P : (t + 1) * P],
+                            rhs=ind[:],
+                            start=True,
+                            stop=True,
+                        )
                 for y in range(2):
                     c = (t % 2) * 256 + y * P
                     nc.tensor.transpose(
@@ -215,10 +224,10 @@ def tile_qwen3nextattentionforengine_pa_t_kernel(
             st[("up", g, 1)] = ups[1]
 
         def stage_rd(g):
-            ssv = stp.tile([P, GT * 2], F32, name="ssv")
+            ssv = stp.tile([P, VT * 4], F32, name="ssv")
             nc.vector.tensor_reduce(
                 out=ssv[:],
-                in_=st[("sq", g, 1)][:].rearrange("p (n j) -> p n j", j=D),
+                in_=st[("sk", g)][:].rearrange("p (n j) -> p n j", j=D),
                 axis=mybir.AxisListType.X,
                 op=ALU.add,
             )
@@ -226,16 +235,15 @@ def tile_qwen3nextattentionforengine_pa_t_kernel(
 
         def stage_r(g):
             rstd = stp.tile([P, GT * 4], F32, name="rstd")
-            rv = rstd[:].rearrange("p (t y h) -> p t y h", y=2, h=2)
             nc.scalar.activation(
-                out=rv[:, :, 0, :],
-                in_=st[("ssp", g)][:].rearrange("p (t n) -> p t n", n=NIND)[:, :, 0:2],
+                out=rstd[:, 0 : PT * 4].rearrange("p (k h) -> p k h", h=2),
+                in_=st[("ssp", g)][:].rearrange("p (k n) -> p k n", n=NIND)[:, :, 0:2],
                 func=ACT.Abs_reciprocal_sqrt,
                 bias=eps_t[:, 0:1],
             )
             nc.scalar.activation(
-                out=rv[:, :, 1, :],
-                in_=st[("ssv", g)][:].rearrange("p (t h) -> p t h", h=2),
+                out=rstd[:, PT * 4 : GT * 4],
+                in_=st[("ssv", g)][:],
                 func=ACT.Abs_reciprocal_sqrt,
                 scale=1.0 / D,
                 bias=eps_t[:, 0:1],

from contextlib import ExitStack

import concourse.mybir as mybir
from concourse.masks import make_identity

F32 = mybir.dt.float32
BF16 = mybir.dt.bfloat16
U32 = mybir.dt.uint32
U8 = mybir.dt.uint8
FP8X4 = mybir.dt.float8_e4m3fn_x4
ALU = mybir.AluOpType
ACT = mybir.ActivationFunctionType

P = 128
HID = 512
D = 64
HALF = 32
NT = 64
GT = 4
NG = NT // GT
CST = 16
GPC = CST // GT
EPS = 1e-6
VT = 1
PT = GT - VT
NIND = 48
FLOPS = 2 * 8192 * 512 * 256


def tile_qwen3nextattentionforengine_pa_t_kernel(
    tc, hidden_states, cos, sin, Wq_query, Wk, q_norm_w, k_norm_w, out_0, out_1
):
    nc = tc.nc
    x_v = hidden_states.rearrange("b (s c) k -> (b s) c k", c=NT)
    cos_v = cos.rearrange("b (s c) j -> (b s) c j", c=NT)
    sin_v = sin.rearrange("b (s c) j -> (b s) c j", c=NT)
    out_v = [
        out_0.rearrange("b (s c) h d -> (b s) c (h d)", c=NT),
        out_1.rearrange("b (s c) h d -> (b s) c (h d)", c=NT),
    ]

    with ExitStack() as ctx:
        const = ctx.enter_context(tc.tile_pool(name="const", bufs=1))
        xp = ctx.enter_context(tc.tile_pool(name="xp", bufs=NG))
        csp = ctx.enter_context(tc.tile_pool(name="csp", bufs=NT // CST))
        grp = ctx.enter_context(tc.tile_pool(name="grp", bufs=3))
        cdp = ctx.enter_context(tc.tile_pool(name="cdp", bufs=3))
        sqp = ctx.enter_context(tc.tile_pool(name="sqp", bufs=4))
        stp = ctx.enter_context(tc.tile_pool(name="stp", bufs=4))
        ttp = ctx.enter_context(tc.tile_pool(name="ttp", bufs=3))
        outp = ctx.enter_context(tc.tile_pool(name="outp", bufs=4))
        ps_t = ctx.enter_context(tc.psum_pool(name="ps_t", bufs=2))
        ps_v = ctx.enter_context(tc.psum_pool(name="ps_v", bufs=2))
        ps_u = ctx.enter_context(tc.psum_pool(name="ps_u", bufs=2))
        ps_k = ctx.enter_context(tc.psum_pool(name="ps_k", bufs=1))
        ps_s = ctx.enter_context(tc.psum_pool(name="ps_s", bufs=1))
        ctx.enter_context(tc.manual_schedule())

        eps_t = const.tile([P, 1], F32)
        nc.vector.memset(eps_t[:], EPS)
        ident = const.tile([P, P], F32)
        make_identity(nc, ident[:])
        ident_b = const.tile([P, P], BF16)
        make_identity(nc, ident_b[:])
        zrow = const.tile([P, P], BF16)
        nc.vector.memset(zrow[:], 0.0)
        ind = const.tile([P, NIND], F32)
        nc.vector.memset(ind[:], 0.0)
        nc.vector.memset(ind[0:D, 0:1], 1.0 / D)
        nc.vector.memset(ind[D:P, 1:2], 1.0 / D)

        w_sb = const.tile([P, 2 * HID], BF16)
        nc.scalar.dma_start(out=w_sb[:, 0:HID], in_=Wq_query)
        nc.scalar.dma_start(out=w_sb[:, HID : 2 * HID], in_=Wk)
        for y, gain in enumerate((q_norm_w, k_norm_w)):
            row = gain.rearrange("(o d) -> o d", o=1)
            nc.scalar.dma_start(out=zrow[y : y + 1, 0:D], in_=row)
            nc.scalar.dma_start(out=zrow[y : y + 1, D:P], in_=row)
        warm = const.tile([P, 1], F32)
        nc.scalar.activation(out=warm[:], in_=eps_t[:], func=ACT.Abs_reciprocal_sqrt)

        x_sb = []
        cs_sb = []
        sraw_sb = []
        for g in range(NG):
            xg = xp.tile([P, GT * HID], BF16, name="xg")
            nc.sync.dma_start(
                out=xg[:].rearrange("p (c k) -> p c k", c=GT), in_=x_v[:, g * GT : (g + 1) * GT, :]
            )
            x_sb.append(xg)
            if g % GPC == 0:
                c0 = g * GT
                cs = csp.tile([P, 2 * CST * D], BF16, name="cs")
                nc.sync.dma_start(
                    out=cs[:, 0 : CST * D].rearrange("p (c j) -> p c j", c=CST),
                    in_=cos_v[:, c0 : c0 + CST, :],
                )
                sraw = csp.tile([P, CST * D], BF16, name="sraw")
                nc.sync.dma_start(
                    out=sraw[:].rearrange("p (c j) -> p c j", c=CST), in_=sin_v[:, c0 : c0 + CST, :]
                )
                cs_sb.append(cs)
                sraw_sb.append(sraw)

        w_f = w_sb[:].bitcast(F32)
        wt = ps_t.tile([P, 512], F32, name="xt")
        for i in range(4):
            nc.tensor.transpose(wt[:, i * P : (i + 1) * P], w_f[:, i * P : (i + 1) * P], ident[:])
        w_gr = const.tile([P, 1024], BF16, align_bytes=64)
        nc.vector.tensor_copy(
            out=w_gr[:].bitcast(F32).rearrange("p (t f u) -> p t f u", t=2, u=2),
            in_=wt[:].rearrange("p (t u f) -> p t f u", t=2, u=2),
        )
        w_codes = const.tile([P, 256], U32, align_bytes=64)
        w_scales = const.tile([P, 256], U8, align_bytes=64)
        nc.vector.quantize_mx(out=w_codes[:].bitcast(FP8X4), scales=w_scales[:], in_=w_gr[:])

        gt_ps = ps_t.tile([P, P], BF16, name="xt")
        nc.tensor.transpose(gt_ps[:], zrow[:], ident_b[:])
        wcol = const.tile([P, 2], F32)
        nc.vector.tensor_copy(out=wcol[:], in_=gt_ps[:, 0:2])

        st = {}

        def stage_cs(k):
            dst = cs_sb[k][:, CST * D : 2 * CST * D].rearrange("p (c j) -> p c j", c=CST)
            src = sraw_sb[k][:].rearrange("p (c j) -> p c j", c=CST)
            nc.gpsimd.tensor_scalar(
                out=dst[:, :, 0:HALF], in0=src[:, :, HALF:D], scalar1=1.0, scalar2=0.0,
                op0=ALU.mult, op1=ALU.add,
            )
            nc.gpsimd.tensor_scalar(
                out=dst[:, :, HALF:D], in0=src[:, :, 0:HALF], scalar1=-1.0, scalar2=0.0,
                op0=ALU.mult, op1=ALU.add,
            )

        def stage_a(g):
            x_f = x_sb[g][:].bitcast(F32)
            for h in range(2):
                xt = ps_t.tile([P, 512], F32, name="xt")
                for i in range(4):
                    c = h * 512 + i * P
                    nc.tensor.transpose(xt[:, i * P : (i + 1) * P], x_f[:, c : c + P], ident[:])
                st[("xt", g, h)] = xt

        def stage_b(g):
            gr = grp.tile([P, GT * 512], BF16, name="gr", align_bytes=64)
            gr_f = gr[:].bitcast(F32)
            for h in range(2):
                nc.scalar.copy(
                    out=gr_f[:, h * 512 : (h + 1) * 512].rearrange("p (t r u) -> p t r u", t=2, u=2),
                    in_=st[("xt", g, h)][:].rearrange("p (t u r) -> p t r u", t=2, u=2),
                )
            st[("gr", g)] = gr

        def stage_c(g):
            codes = cdp.tile([P, GT * P], U32, name="codes", align_bytes=64)
            scales = cdp.tile([P, GT * P], U8, name="scales", align_bytes=64)
            nc.vector.quantize_mx(out=codes[:].bitcast(FP8X4), scales=scales[:], in_=st[("gr", g)][:])
            st[("cd", g)] = (codes, scales)

        def stage_d(g):
            codes, scales = st[("cd", g)]
            for y in range(2):
                vt = ps_v.tile([P, 512], F32, name="vt")
                nc.tensor.matmul_mx(
                    out=vt[:],
                    lhsT=w_codes[:, y * P : (y + 1) * P].bitcast(FP8X4),
                    lhsT_scale=w_scales[:, y * P : (y + 1) * P],
                    rhs=codes[:].bitcast(FP8X4),
                    rhs_scale=scales[:],
                    start=True,
                    stop=True,
                )
                st[("vt", g, y)] = vt
            mk = ps_k.tile([P, VT * 256], F32, name="mk")
            for v in range(VT):
                c = (PT + v) * P
                nc.tensor.matmul_mx(
                    out=mk[:, v * 256 : (v + 1) * 256],
                    lhsT=codes[:, c : c + P].bitcast(FP8X4),
                    lhsT_scale=scales[:, c : c + P],
                    rhs=w_codes[:].bitcast(FP8X4),
                    rhs_scale=w_scales[:],
                    start=True,
                    stop=True,
                )
            st[("mk", g)] = mk

        def stage_e(g):
            for y in range(2):
                vt = st[("vt", g, y)]
                sq = sqp.tile([P, PT * P], F32, name="sq")
                nc.scalar.activation(out=sq[:], in_=vt[:, 0 : PT * P], func=ACT.Square)
                ut = sqp.tile([P, 512], F32, name="ut")
                nc.scalar.activation(out=ut[:], in_=vt[:], func=ACT.Copy, scale=wcol[:, y : y + 1])
                st[("sq", g, y)] = sq
                st[("ut", g, y)] = ut
            sk = sqp.tile([P, VT * 256], F32, name="sk")
            nc.scalar.activation(out=sk[:], in_=st[("mk", g)][:], func=ACT.Square)
            st[("sk", g)] = sk

        def stage_mt(g):
            ssp = ps_s.tile([P, 2 * PT * NIND], F32, name="ssp")
            ups = [ps_u.tile([P, 512], F32, name="up") for hb in range(2)]
            for t in range(GT):
                for y in range(2):
                    if t < PT:
                        k = t * 2 + y
                        nc.tensor.matmul(
                            out=ssp[:, k * NIND : (k + 1) * NIND],
                            lhsT=st[("sq", g, y)][:, t * P : (t + 1) * P],
                            rhs=ind[:],
                            start=True,
                            stop=True,
                        )
                for y in range(2):
                    c = (t % 2) * 256 + y * P
                    nc.tensor.transpose(
                        ups[t // 2][:, c : c + P], st[("ut", g, y)][:, t * P : (t + 1) * P], ident[:]
                    )
            st[("ssp", g)] = ssp
            st[("up", g, 0)] = ups[0]
            st[("up", g, 1)] = ups[1]

        def stage_rd(g):
            ssv = stp.tile([P, VT * 4], F32, name="ssv")
            nc.vector.tensor_reduce(
                out=ssv[:],
                in_=st[("sk", g)][:].rearrange("p (n j) -> p n j", j=D),
                axis=mybir.AxisListType.X,
                op=ALU.add,
            )
            st[("ssv", g)] = ssv

        def stage_r(g):
            rstd = stp.tile([P, GT * 4], F32, name="rstd")
            nc.scalar.activation(
                out=rstd[:, 0 : PT * 4].rearrange("p (k h) -> p k h", h=2),
                in_=st[("ssp", g)][:].rearrange("p (k n) -> p k n", n=NIND)[:, :, 0:2],
                func=ACT.Abs_reciprocal_sqrt,
                bias=eps_t[:, 0:1],
            )
            nc.scalar.activation(
                out=rstd[:, PT * 4 : GT * 4],
                in_=st[("ssv", g)][:],
                func=ACT.Abs_reciprocal_sqrt,
                scale=1.0 / D,
                bias=eps_t[:, 0:1],
            )
            st[("rstd", g)] = rstd

        def stage_f(g):
            rstd = st[("rstd", g)]
            tt = ttp.tile([P, GT * 4 * 2 * D], F32, name="tt")
            csv = cs_sb[g // GPC][:].rearrange("p (r c j) -> p r c j", r=2, c=CST)
            for hb in range(2):
                up = st[("up", g, hb)]
                for t2 in range(2):
                    t = hb * 2 + t2
                    for yh in range(4):
                        si = t * 4 + yh
                        ti = (yh // 2) * 8 + t * 2 + yh % 2
                        c = t2 * 256 + yh * D
                        nc.vector.scalar_tensor_tensor(
                            out=tt[:, ti * 128 : (ti + 1) * 128].rearrange("p (r j) -> p r j", r=2),
                            in0=up[:, c : c + D].unsqueeze(1).to_broadcast([P, 2, D]),
                            scalar=rstd[:, si : si + 1],
                            in1=csv[:, :, (g % GPC) * GT + t, :],
                            op0=ALU.mult,
                            op1=ALU.mult,
                        )
            st[("tt", g)] = tt

        def stage_h(g):
            ttv = st[("tt", g)][:].rearrange("p (n r j) -> p n r j", r=2, j=D)
            o = outp.tile([P, 2 * GT * 128], F32, name="o")
            ov = o[:].rearrange("p (n j) -> p n j", j=D)
            for half in range(2):
                a = half * HALF
                b = (1 - half) * HALF
                nc.gpsimd.tensor_tensor(
                    out=ov[:, :, a : a + HALF],
                    in0=ttv[:, :, 0, a : a + HALF],
                    in1=ttv[:, :, 1, b : b + HALF],
                    op=ALU.add,
                )
            for y in range(2):
                nc.sync.dma_start(
                    out=out_v[y][:, g * GT : (g + 1) * GT, :],
                    in_=o[:, y * GT * 128 : (y + 1) * GT * 128].rearrange("p (t f) -> p t f", t=GT),
                )

        def on(g):
            return 0 <= g < NG

        for i in range(NG + 5):
            if i % GPC == 0 and i < NG:
                stage_cs(i // GPC)
            if on(i - 3):
                stage_e(i - 3)
            if on(i - 4):
                stage_rd(i - 4)
                stage_r(i - 4)
            if on(i - 5):
                stage_f(i - 5)
            if on(i - 2):
                stage_c(i - 2)
                stage_d(i - 2)
            if on(i - 1):
                stage_b(i - 1)
            if on(i - 3):
                stage_mt(i - 3)
            if on(i):
                stage_a(i)
            if on(i - 5):
                stage_h(i - 5)
